import numpy as np
import ml_dtypes


def mxq(x, axis, fmt="e4m3"):
    dtype, down = {"e4m3": (ml_dtypes.float8_e4m3fn, 7), "e5m2": (ml_dtypes.float8_e5m2, 14)}[fmt]
    v = np.moveaxis(np.asarray(x, np.float32).astype(ml_dtypes.bfloat16).astype(np.float64), axis, -1)
    blocks = v.reshape(v.shape[:-1] + (-1, 32))
    amax = np.abs(blocks).max(-1, keepdims=True)
    byte = np.maximum(np.where(amax > 0, np.frexp(amax)[1] - 1 + 127, 0) - down, 1)
    scale = np.exp2(byte - 127.0)
    codes = (blocks / scale).astype(np.float32).astype(dtype).astype(np.float64)
    return np.moveaxis((codes * scale).reshape(v.shape), -1, axis)


WIDE = False


def mx_kscale(k):
    if not WIDE:
        return np.ones(k)
    levels = np.array([10, -10, 5, -5, 0])
    a = np.random.permutation(np.resize(levels, k // 512 * 4)).reshape(k // 512, 4)
    idx = np.arange(k)
    return np.exp2(a[idx // 512, idx % 128 // 32])


BF16 = ml_dtypes.bfloat16


def bf(x):
    return np.asarray(x, np.float32).astype(BF16)


def f64(x):
    return np.asarray(x).astype(np.float64)


B, S, D, H, KVH, DH, F = 2, 256, 1024, 8, 2, 128, 4096
EPS = 1e-6
E = H * DH


def rms_norm(v, eps):
    return v / np.sqrt(np.mean(np.square(v), axis=-1, keepdims=True) + eps)


def setup_inputs():
    s = mx_kscale(E)
    return {"y_attn": bf(np.random.standard_normal((B, H, S, DH)) * 0.35 * s.reshape(H, 1, DH)),
            "x": bf(np.random.standard_normal((B, S, D))),
            "w_o": bf(np.random.standard_normal((D, E)) / np.sqrt(E) / s[None, :]),
            "attn_scale": bf(1.0 + 0.1 * np.random.standard_normal(D)),
            "w_fc": bf(np.random.standard_normal((F, D)) / np.sqrt(D))}


def reference(y_attn, x, w_o, attn_scale, w_fc):
    yc = f64(y_attn).transpose(0, 2, 1, 3).reshape(B, S, E)
    attn_out = mxq(yc, 2, "e4m3") @ mxq(f64(w_o), 1, "e4m3").T
    x_mid = f64(x) + f64(attn_scale)[None, None, :] * attn_out
    h = mxq(rms_norm(x_mid, EPS), 2, "e4m3") @ mxq(f64(w_fc), 1, "e4m3").T
    h = np.square(np.maximum(h, 0.0))
    return x_mid, h

@@ -1,0 +1,239 @@
+from contextlib import ExitStack
+
+import concourse.mybir as mybir
+from concourse.masks import make_identity
+
+F32 = mybir.dt.float32
+BF16 = mybir.dt.bfloat16
+U32 = mybir.dt.uint32
+U8 = mybir.dt.uint8
+FP8X4 = mybir.dt.float8_e4m3fn_x4
+ALU = mybir.AluOpType
+ACT = mybir.ActivationFunctionType
+
+P = 128
+SEQ = 256
+HEADS = 8
+TOKENS = 512
+MODEL = 1024
+HIDDEN = 4096
+EPS = 1e-6
+
+PACK = 4
+K_PASS = P * PACK
+PASSES = MODEL // K_PASS
+HALVES = 2
+TOKEN_TILES = TOKENS // P
+N_TILE = 512
+UNIT_ROWS = 2 * P
+UNITS_PER_CHUNK = N_TILE // UNIT_ROWS
+WO_UNITS = MODEL // UNIT_ROWS
+WFC_UNITS = HIDDEN // UNIT_ROWS
+STORE_COLS = 1024
+UNITS_AHEAD = 8
+VECTOR_EVERY = 4
+
+FLOPS = 2 * TOKENS * MODEL * (MODEL + HIDDEN)
+
+
+def tile_shepherdembryo_pb_kernel(tc, y_attn, x, w_o, attn_scale, w_fc, out_0, out_1):
+    nc = tc.nc
+    x_rows = x.flatten_outer_dims()
+    x_mid_rows = out_0.flatten_outer_dims()
+    h_rows = out_1.flatten_outer_dims()
+
+    with ExitStack() as ctx:
+        consts = ctx.enter_context(tc.tile_pool(name="consts", bufs=1))
+        inputs = ctx.enter_context(tc.tile_pool(name="inputs", bufs=1))
+        weights = ctx.enter_context(tc.tile_pool(name="weights", bufs=WFC_UNITS))
+        packed = ctx.enter_context(tc.tile_pool(name="packed", bufs=1))
+        stage = ctx.enter_context(tc.tile_pool(name="stage", bufs=6))
+        norm = ctx.enter_context(tc.tile_pool(name="norm", bufs=2))
+        mids = ctx.enter_context(tc.tile_pool(name="mids", bufs=TOKEN_TILES))
+        hidden = ctx.enter_context(tc.tile_pool(name="hidden", bufs=6))
+        psum = ctx.enter_context(tc.psum_pool(name="psum", bufs=4))
+
+        eps_col = consts.tile([P, 1], F32)
+        nc.vector.memset(eps_col[:], EPS)
+        table_warmer = consts.tile([P, 1], F32)
+        nc.scalar.activation(out=table_warmer[:], in_=eps_col[:], func=ACT.Sqrt)
+
+        ident_words = consts.tile([P, P], F32)
+        make_identity(nc, ident_words[:])
+        ident_bf16 = consts.tile([P, P], BF16)
+        make_identity(nc, ident_bf16[:])
+
+        gain_row0 = consts.tile([P, MODEL], BF16)
+        nc.vector.memset(gain_row0[:], 0.0)
+        nc.scalar.dma_start(out=gain_row0[0:1, :], in_=attn_scale.rearrange("(o d) -> o d", o=1))
+        ones = consts.tile([P, P], BF16)
+        nc.vector.memset(ones[:], 1.0)
+
+        def load_tokens(tt):
+            b, s0 = divmod(tt * P, SEQ)
+            y_sb = inputs.tile([P, MODEL], BF16, name="y_sb%d" % tt)
+            nc.sync.dma_start(
+                out=y_sb[:].rearrange("s (h j) -> s h j", h=HEADS),
+                in_=y_attn[b, :, s0 : s0 + P, :].rearrange("h s j -> s h j"),
+            )
+            return y_sb
+
+        def load_unit(w, unit):
+            raw = weights.tile([P, 2, MODEL], BF16, tag="raw")
+            nc.sync.dma_start(
+                out=raw[:].rearrange("p r k -> p (r k)"),
+                in_=w[unit * UNIT_ROWS : (unit + 1) * UNIT_ROWS, :].rearrange("(p r) k -> p (r k)", r=2),
+            )
+            return raw
+
+        def copy_words_out(bank_number, out, in_):
+            if bank_number % VECTOR_EVERY == 0:
+                nc.vector.tensor_copy(out=out, in_=in_)
+            else:
+                nc.scalar.copy(out=out, in_=in_)
+
+        def quantise_tokens(tt, y_sb, codes, scales):
+            words = y_sb[:].bitcast(F32)
+            bank = psum.tile([P, PASSES, HALVES, P], F32, tag="flip")
+            for g in range(PASSES):
+                for u in range(HALVES):
+                    first = (HALVES * g + u) * P
+                    nc.tensor.transpose(bank[:, g, u, :], words[:, first : first + P], ident_words[:])
+            grouped = stage.tile([P, PASSES * P * PACK], BF16, tag="grouped", align_bytes=64)
+            copy_words_out(
+                tt,
+                out=grouped[:].bitcast(F32).rearrange("p (g t u) -> p g t u", g=PASSES, u=HALVES),
+                in_=bank[:].rearrange("p g u t -> p g t u"),
+            )
+            nc.vector.quantize_mx(out=codes[:].bitcast(FP8X4), scales=scales[:], in_=grouped[:])
+
+        def quantise_unit(unit, raw, codes, scales):
+            words = raw[:].bitcast(F32)
+            first_col = (unit % UNITS_PER_CHUNK) * UNIT_ROWS
+            cols = slice(first_col, first_col + UNIT_ROWS)
+            for g in range(PASSES):
+                bank = psum.tile([P, HALVES, 2, P], F32, tag="flip")
+                for u in range(HALVES):
+                    first = (HALVES * g + u) * P
+                    for r in range(2):
+                        nc.tensor.transpose(bank[:, u, r, :], words[:, r, first : first + P], ident_words[:])
+                grouped = stage.tile([P, UNIT_ROWS * PACK], BF16, tag="grouped", align_bytes=64)
+                copy_words_out(
+                    PASSES * unit + g,
+                    out=grouped[:].bitcast(F32).rearrange("p (q r u) -> p q r u", r=2, u=HALVES),
+                    in_=bank[:].rearrange("p u r q -> p q r u"),
+                )
+                nc.vector.quantize_mx(
+                    out=codes[:, g, cols].bitcast(FP8X4), scales=scales[:, g, cols], in_=grouped[:]
+                )
+
+        def packed_tokens(name):
+            codes = packed.tile([P, PASSES * P], U32, name=name + "_codes", align_bytes=64)
+            scales = packed.tile([P, PASSES * P], U8, name=name + "_scales", align_bytes=64)
+            return codes, scales
+
+        def packed_chunk(name):
+            codes = packed.tile([P, PASSES, N_TILE], U32, name=name + "_codes", align_bytes=64)
+            scales = packed.tile([P, PASSES, N_TILE], U8, name=name + "_scales", align_bytes=64)
+            return codes, scales
+
+        def multiply(tokens, chunk):
+            t_codes, t_scales = tokens
+            c_codes, c_scales = chunk
+            acc = psum.tile([P, N_TILE], F32, tag="acc")
+            for g in range(PASSES):
+                t_cols = slice(g * P, (g + 1) * P)
+                nc.tensor.matmul_mx(
+                    out=acc[:],
+                    lhsT=t_codes[:, t_cols].bitcast(FP8X4),
+                    lhsT_scale=t_scales[:, t_cols],
+                    rhs=c_codes[:, g, :].bitcast(FP8X4),
+                    rhs_scale=c_scales[:, g, :],
+                    start=(g == 0),
+                    stop=(g == PASSES - 1),
+                )
+            return acc
+
+        y_tiles = [load_tokens(tt) for tt in range(TOKEN_TILES)]
+        wo_raw = [load_unit(w_o, unit) for unit in range(WO_UNITS)]
+        x_sb = inputs.tile([P, TOKEN_TILES, MODEL], BF16)
+        nc.sync.dma_start(out=x_sb[:], in_=x_rows.rearrange("(t p) d -> p t d", p=P))
+
+        yc = [packed_tokens("yc%d" % tt) for tt in range(TOKEN_TILES)]
+        for tt in range(TOKEN_TILES):
+            quantise_tokens(tt, y_tiles[tt], yc[tt][0], yc[tt][1])
+
+        wo = [packed_chunk("wo%d" % c) for c in range(WO_UNITS // UNITS_PER_CHUNK)]
+        for unit in range(WO_UNITS):
+            chunk = wo[unit // UNITS_PER_CHUNK]
+            quantise_unit(unit, wo_raw[unit], chunk[0], chunk[1])
+
+        wfc_raw = [load_unit(w_fc, unit) for unit in range(WFC_UNITS)]
+
+        gain = consts.tile([P, MODEL], BF16)
+        for dc in range(MODEL // N_TILE):
+            cols = slice(dc * N_TILE, (dc + 1) * N_TILE)
+            spread = psum.tile([P, N_TILE], F32, tag="acc")
+            nc.tensor.matmul(out=spread[:], lhsT=ones[:], rhs=gain_row0[:, cols], start=True, stop=True)
+            nc.vector.tensor_copy(out=gain[:, cols], in_=spread[:])
+
+        xn = [packed_tokens("xn%d" % tt) for tt in range(TOKEN_TILES)]
+        for tt in range(TOKEN_TILES):
+            gained = norm.tile([P, MODEL], F32, tag="gained")
+            for dc in range(MODEL // N_TILE):
+                cols = slice(dc * N_TILE, (dc + 1) * N_TILE)
+                attn_out = multiply(yc[tt], wo[dc])
+                nc.vector.tensor_tensor(out=gained[:, cols], in0=attn_out[:], in1=gain[:, cols], op=ALU.mult)
+            x_mid = mids.tile([P, MODEL], F32, tag="x_mid")
+            nc.vector.tensor_tensor(out=x_mid[:], in0=gained[:], in1=x_sb[:, tt, :], op=ALU.add)
+            nc.sync.dma_start(out=x_mid_rows[tt * P : (tt + 1) * P, :], in_=x_mid[:])
+
+            squares = norm.tile([P, MODEL], BF16, tag="squares")
+            mean_sq = norm.tile([P, 1], F32, tag="mean_sq")
+            nc.scalar.activation(
+                out=squares[:], in_=x_mid[:], func=ACT.Square, scale=MODEL**-0.5, accum_out=mean_sq[:]
+            )
+            rms = norm.tile([P, 1], F32, tag="rms")
+            nc.scalar.activation(out=rms[:], in_=mean_sq[:], func=ACT.Sqrt, bias=eps_col[:])
+            inv_rms = norm.tile([P, 1], F32, tag="inv_rms")
+            nc.vector.reciprocal(out=inv_rms[:], in_=rms[:])
+
+            xn_sorted = norm.tile([P, PASSES * HALVES, 2, P], BF16, tag="xn_sorted")
+            nc.scalar.activation(
+                out=xn_sorted[:],
+                in_=x_mid[:].rearrange("t (a p e) -> t a e p", p=P, e=2),
+                func=ACT.Copy,
+                scale=inv_rms[:],
+            )
+            bank = psum.tile([P, PASSES, PACK, P], BF16, tag="flip")
+            for g in range(PASSES):
+                for u in range(HALVES):
+                    for e in range(2):
+                        nc.tensor.transpose(bank[:, g, 2 * u + e, :], xn_sorted[:, HALVES * g + u, e, :], ident_bf16[:])
+            grouped = stage.tile([P, PASSES * P * PACK], BF16, tag="grouped", align_bytes=64)
+            nc.scalar.copy(
+                out=grouped[:].rearrange("p (g t v) -> p g t v", g=PASSES, v=PACK),
+                in_=bank[:].rearrange("p g v t -> p g t v"),
+            )
+            nc.vector.quantize_mx(out=xn[tt][0][:].bitcast(FP8X4), scales=xn[tt][1][:], in_=grouped[:])
+
+        wfc = [packed_chunk("wfc%d" % c) for c in range(WFC_UNITS // UNITS_PER_CHUNK)]
+
+        def quantise_wfc_unit(unit):
+            chunk = wfc[unit // UNITS_PER_CHUNK]
+            quantise_unit(unit, wfc_raw[unit], chunk[0], chunk[1])
+
+        def up_project(tt, first_col):
+            h_sb = hidden.tile([P, STORE_COLS], F32, tag="h_sb")
+            for col in range(0, STORE_COLS, N_TILE):
+                product = multiply(xn[tt], wfc[(first_col + col) // N_TILE])
+                nc.scalar.activation(out=h_sb[:, col : col + N_TILE], in_=product[:], func=ACT.Relu)
+            nc.vector.tensor_tensor(out=h_sb[:], in0=h_sb[:], in1=h_sb[:], op=ALU.mult)
+            nc.sync.dma_start(out=h_rows[tt * P : (tt + 1) * P, first_col : first_col + STORE_COLS], in_=h_sb[:])
+
+        for unit in range(UNITS_AHEAD):
+            quantise_wfc_unit(unit)
+        for step in range(WFC_UNITS):
+            if step + UNITS_AHEAD < WFC_UNITS:
+                quantise_wfc_unit(step + UNITS_AHEAD)
+            up_project(step % TOKEN_TILES, (step // TOKEN_TILES) * STORE_COLS)

@@ -29,8 +29,8 @@ UNIT_ROWS = 2 * P
 UNITS_PER_CHUNK = N_TILE // UNIT_ROWS
 WO_UNITS = MODEL // UNIT_ROWS
 WFC_UNITS = HIDDEN // UNIT_ROWS
-STORE_COLS = 1024
-UNITS_AHEAD = 8
+PIECE_COLS = 1024
+PIECES = TOKEN_TILES * (HIDDEN // PIECE_COLS)
 VECTOR_EVERY = 4
 
 FLOPS = 2 * TOKENS * MODEL * (MODEL + HIDDEN)
@@ -52,31 +52,21 @@ def tile_shepherdembryo_pb_kernel(tc, y_attn, x, w_o, attn_scale, w_fc, out_0, o
         mids = ctx.enter_context(tc.tile_pool(name="mids", bufs=TOKEN_TILES))
         hidden = ctx.enter_context(tc.tile_pool(name="hidden", bufs=6))
         psum = ctx.enter_context(tc.psum_pool(name="psum", bufs=4))
-
-        eps_col = consts.tile([P, 1], F32)
-        nc.vector.memset(eps_col[:], EPS)
-        table_warmer = consts.tile([P, 1], F32)
-        nc.scalar.activation(out=table_warmer[:], in_=eps_col[:], func=ACT.Sqrt)
-
-        ident_words = consts.tile([P, P], F32)
-        make_identity(nc, ident_words[:])
-        ident_bf16 = consts.tile([P, P], BF16)
-        make_identity(nc, ident_bf16[:])
+        ctx.enter_context(tc.manual_schedule())
 
         gain_row0 = consts.tile([P, MODEL], BF16)
         nc.vector.memset(gain_row0[:], 0.0)
         nc.scalar.dma_start(out=gain_row0[0:1, :], in_=attn_scale.rearrange("(o d) -> o d", o=1))
         ones = consts.tile([P, P], BF16)
         nc.vector.memset(ones[:], 1.0)
-
-        def load_tokens(tt):
-            b, s0 = divmod(tt * P, SEQ)
-            y_sb = inputs.tile([P, MODEL], BF16, name="y_sb%d" % tt)
-            nc.sync.dma_start(
-                out=y_sb[:].rearrange("s (h j) -> s h j", h=HEADS),
-                in_=y_attn[b, :, s0 : s0 + P, :].rearrange("h s j -> s h j"),
-            )
-            return y_sb
+        eps_col = consts.tile([P, 1], F32)
+        nc.vector.memset(eps_col[:], EPS)
+        table_warmer = consts.tile([P, 1], F32)
+        nc.scalar.activation(out=table_warmer[:], in_=eps_col[:], func=ACT.Sqrt)
+        ident_words = consts.tile([P, P], F32)
+        make_identity(nc, ident_words[:])
+        ident_bf16 = consts.tile([P, P], BF16)
+        make_identity(nc, ident_bf16[:])
 
         def load_unit(w, unit):
             raw = weights.tile([P, 2, MODEL], BF16, tag="raw")
@@ -86,46 +76,24 @@ def tile_shepherdembryo_pb_kernel(tc, y_attn, x, w_o, attn_scale, w_fc, out_0, o
             )
             return raw
 
-        def copy_words_out(bank_number, out, in_):
-            if bank_number % VECTOR_EVERY == 0:
-                nc.vector.tensor_copy(out=out, in_=in_)
-            else:
-                nc.scalar.copy(out=out, in_=in_)
-
-        def quantise_tokens(tt, y_sb, codes, scales):
-            words = y_sb[:].bitcast(F32)
-            bank = psum.tile([P, PASSES, HALVES, P], F32, tag="flip")
-            for g in range(PASSES):
-                for u in range(HALVES):
-                    first = (HALVES * g + u) * P
-                    nc.tensor.transpose(bank[:, g, u, :], words[:, first : first + P], ident_words[:])
-            grouped = stage.tile([P, PASSES * P * PACK], BF16, tag="grouped", align_bytes=64)
-            copy_words_out(
-                tt,
-                out=grouped[:].bitcast(F32).rearrange("p (g t u) -> p g t u", g=PASSES, u=HALVES),
-                in_=bank[:].rearrange("p g u t -> p g t u"),
+        def load_tokens(tt):
+            b, s0 = divmod(tt * P, SEQ)
+            y_sb = inputs.tile([P, MODEL], BF16, name="y_sb%d" % tt)
+            nc.sync.dma_start(
+                out=y_sb[:].rearrange("s (h j) -> s h j", h=HEADS),
+                in_=y_attn[b, :, s0 : s0 + P, :].rearrange("h s j -> s h j"),
             )
-            nc.vector.quantize_mx(out=codes[:].bitcast(FP8X4), scales=scales[:], in_=grouped[:])
+            x_sb = inputs.tile([P, MODEL], BF16, name="x_sb%d" % tt)
+            nc.sync.dma_start(out=x_sb[:], in_=x_rows[tt * P : (tt + 1) * P, :])
+            return y_sb, x_sb
 
-        def quantise_unit(unit, raw, codes, scales):
-            words = raw[:].bitcast(F32)
-            first_col = (unit % UNITS_PER_CHUNK) * UNIT_ROWS
-            cols = slice(first_col, first_col + UNIT_ROWS)
-            for g in range(PASSES):
-                bank = psum.tile([P, HALVES, 2, P], F32, tag="flip")
-                for u in range(HALVES):
-                    first = (HALVES * g + u) * P
-                    for r in range(2):
-                        nc.tensor.transpose(bank[:, u, r, :], words[:, r, first : first + P], ident_words[:])
-                grouped = stage.tile([P, UNIT_ROWS * PACK], BF16, tag="grouped", align_bytes=64)
-                copy_words_out(
-                    PASSES * unit + g,
-                    out=grouped[:].bitcast(F32).rearrange("p (q r u) -> p q r u", r=2, u=HALVES),
-                    in_=bank[:].rearrange("p u r q -> p q r u"),
-                )
-                nc.vector.quantize_mx(
-                    out=codes[:, g, cols].bitcast(FP8X4), scales=scales[:, g, cols], in_=grouped[:]
-                )
+        raw_units = [load_unit(w_o, unit) for unit in range(WO_UNITS)]
+        token_inputs = [load_tokens(tt) for tt in range(2)]
+        for tt in range(2, TOKEN_TILES):
+            raw_units.extend([load_unit(w_fc, unit) for unit in range(2 * tt - 4, 2 * tt - 2)])
+            token_inputs.append(load_tokens(tt))
+        raw_units.extend([load_unit(w_fc, unit) for unit in range(2 * TOKEN_TILES - 4, WFC_UNITS - WO_UNITS)])
+        ALL_UNITS = WO_UNITS + WFC_UNITS
 
         def packed_tokens(name):
             codes = packed.tile([P, PASSES * P], U32, name=name + "_codes", align_bytes=64)
@@ -136,6 +104,12 @@ def tile_shepherdembryo_pb_kernel(tc, y_attn, x, w_o, attn_scale, w_fc, out_0, o
             codes = packed.tile([P, PASSES, N_TILE], U32, name=name + "_codes", align_bytes=64)
             scales = packed.tile([P, PASSES, N_TILE], U8, name=name + "_scales", align_bytes=64)
             return codes, scales
+
+        yc = [packed_tokens("yc%d" % tt) for tt in range(TOKEN_TILES)]
+        xn = [packed_tokens("xn%d" % tt) for tt in range(TOKEN_TILES)]
+        chunks = [packed_chunk("w%d" % c) for c in range(ALL_UNITS // UNITS_PER_CHUNK)]
+        wo = chunks[: WO_UNITS // UNITS_PER_CHUNK]
+        wfc = chunks[WO_UNITS // UNITS_PER_CHUNK :]
 
         def multiply(tokens, chunk):
             t_codes, t_scales = tokens
@@ -154,21 +128,145 @@ def tile_shepherdembryo_pb_kernel(tc, y_attn, x, w_o, attn_scale, w_fc, out_0, o
                 )
             return acc
 
-        y_tiles = [load_tokens(tt) for tt in range(TOKEN_TILES)]
-        wo_raw = [load_unit(w_o, unit) for unit in range(WO_UNITS)]
-        x_sb = inputs.tile([P, TOKEN_TILES, MODEL], BF16)
-        nc.sync.dma_start(out=x_sb[:], in_=x_rows.rearrange("(t p) d -> p t d", p=P))
+        handed = {}
 
-        yc = [packed_tokens("yc%d" % tt) for tt in range(TOKEN_TILES)]
-        for tt in range(TOKEN_TILES):
-            quantise_tokens(tt, y_tiles[tt], yc[tt][0], yc[tt][1])
+        def flip_unit(unit):
+            words = raw_units[unit][:].bitcast(F32)
+            for g in range(PASSES):
+                bank = psum.tile([P, HALVES, 2, P], F32, tag="flip")
+                for u in range(HALVES):
+                    first = (HALVES * g + u) * P
+                    for r in range(2):
+                        nc.tensor.transpose(bank[:, u, r, :], words[:, r, first : first + P], ident_words[:])
+                handed[("unit bank", unit, g)] = bank
 
-        wo = [packed_chunk("wo%d" % c) for c in range(WO_UNITS // UNITS_PER_CHUNK)]
-        for unit in range(WO_UNITS):
-            chunk = wo[unit // UNITS_PER_CHUNK]
-            quantise_unit(unit, wo_raw[unit], chunk[0], chunk[1])
+        def copy_unit(unit):
+            for g in range(PASSES):
+                grouped = stage.tile([P, UNIT_ROWS * PACK], BF16, tag="grouped", align_bytes=64)
+                out = grouped[:].bitcast(F32).rearrange("p (q r u) -> p q r u", r=2, u=HALVES)
+                in_ = handed[("unit bank", unit, g)][:].rearrange("p u r q -> p q r u")
+                if (PASSES * unit + g) % VECTOR_EVERY == 0:
+                    nc.vector.tensor_copy(out=out, in_=in_)
+                else:
+                    nc.scalar.copy(out=out, in_=in_)
+                handed[("unit grouped", unit, g)] = grouped
 
-        wfc_raw = [load_unit(w_fc, unit) for unit in range(WFC_UNITS)]
+        def quantise_unit(unit):
+            codes, scales = chunks[unit // UNITS_PER_CHUNK]
+            first_col = (unit % UNITS_PER_CHUNK) * UNIT_ROWS
+            cols = slice(first_col, first_col + UNIT_ROWS)
+            for g in range(PASSES):
+                nc.vector.quantize_mx(
+                    out=codes[:, g, cols].bitcast(FP8X4),
+                    scales=scales[:, g, cols],
+                    in_=handed[("unit grouped", unit, g)][:],
+                )
+
+        def flip_yc(tt):
+            words = token_inputs[tt][0][:].bitcast(F32)
+            bank = psum.tile([P, PASSES, HALVES, P], F32, tag="flip")
+            for g in range(PASSES):
+                for u in range(HALVES):
+                    first = (HALVES * g + u) * P
+                    nc.tensor.transpose(bank[:, g, u, :], words[:, first : first + P], ident_words[:])
+            handed[("yc bank", tt)] = bank
+
+        def copy_yc(tt):
+            grouped = stage.tile([P, PASSES * P * PACK], BF16, tag="grouped", align_bytes=64)
+            nc.scalar.copy(
+                out=grouped[:].bitcast(F32).rearrange("p (g t u) -> p g t u", g=PASSES, u=HALVES),
+                in_=handed[("yc bank", tt)][:].rearrange("p g u t -> p g t u"),
+            )
+            handed[("yc grouped", tt)] = grouped
+
+        def quantise_yc(tt):
+            nc.vector.quantize_mx(
+                out=yc[tt][0][:].bitcast(FP8X4), scales=yc[tt][1][:], in_=handed[("yc grouped", tt)][:]
+            )
+
+        def project(tt):
+            handed[("attn_out", tt)] = [multiply(yc[tt], wo[dc]) for dc in range(MODEL // N_TILE)]
+
+        def add_residual(tt):
+            gained = norm.tile([P, MODEL], F32, tag="gained")
+            for dc, attn_out in enumerate(handed[("attn_out", tt)]):
+                cols = slice(dc * N_TILE, (dc + 1) * N_TILE)
+                nc.vector.tensor_tensor(out=gained[:, cols], in0=attn_out[:], in1=gain[:, cols], op=ALU.mult)
+            x_mid = mids.tile([P, MODEL], F32, tag="x_mid")
+            nc.vector.tensor_tensor(out=x_mid[:], in0=gained[:], in1=token_inputs[tt][1][:], op=ALU.add)
+            nc.sync.dma_start(out=x_mid_rows[tt * P : (tt + 1) * P, :], in_=x_mid[:])
+            handed[("x_mid", tt)] = x_mid
+
+        def root_mean_square(tt):
+            squares = norm.tile([P, MODEL], BF16, tag="squares")
+            mean_sq = norm.tile([P, 1], F32, tag="mean_sq")
+            nc.scalar.activation(
+                out=squares[:], in_=handed[("x_mid", tt)][:], func=ACT.Square, scale=MODEL**-0.5, accum_out=mean_sq[:]
+            )
+            rms = norm.tile([P, 1], F32, tag="rms")
+            nc.scalar.activation(out=rms[:], in_=mean_sq[:], func=ACT.Sqrt, bias=eps_col[:])
+            handed[("rms", tt)] = rms
+
+        def invert_rms(tt):
+            inv_rms = norm.tile([P, 1], F32, tag="inv_rms")
+            nc.vector.reciprocal(out=inv_rms[:], in_=handed[("rms", tt)][:])
+            handed[("inv_rms", tt)] = inv_rms
+
+        def normalise(tt):
+            xn_sorted = norm.tile([P, PASSES * HALVES, 2, P], BF16, tag="xn_sorted")
+            nc.scalar.activation(
+                out=xn_sorted[:],
+                in_=handed[("x_mid", tt)][:].rearrange("t (a p e) -> t a e p", p=P, e=2),
+                func=ACT.Copy,
+                scale=handed[("inv_rms", tt)][:],
+            )
+            handed[("xn_sorted", tt)] = xn_sorted
+
+        def flip_xn(tt):
+            xn_sorted = handed[("xn_sorted", tt)]
+            bank = psum.tile([P, PASSES, PACK, P], BF16, tag="flip")
+            for g in range(PASSES):
+                for u in range(HALVES):
+                    for e in range(2):
+                        nc.tensor.transpose(bank[:, g, 2 * u + e, :], xn_sorted[:, HALVES * g + u, e, :], ident_bf16[:])
+            handed[("xn bank", tt)] = bank
+
+        def copy_xn(tt):
+            grouped = stage.tile([P, PASSES * P * PACK], BF16, tag="grouped", align_bytes=64)
+            nc.scalar.copy(
+                out=grouped[:].rearrange("p (g t v) -> p g t v", g=PASSES, v=PACK),
+                in_=handed[("xn bank", tt)][:].rearrange("p g v t -> p g t v"),
+            )
+            handed[("xn grouped", tt)] = grouped
+
+        def quantise_xn(tt):
+            nc.vector.quantize_mx(
+                out=xn[tt][0][:].bitcast(FP8X4), scales=xn[tt][1][:], in_=handed[("xn grouped", tt)][:]
+            )
+
+        def place_of_piece(piece):
+            return piece % TOKEN_TILES, (piece // TOKEN_TILES) * PIECE_COLS
+
+        def up_multiply(piece):
+            tt, first_col = place_of_piece(piece)
+            first_chunk = first_col // N_TILE
+            handed[("product", piece)] = [multiply(xn[tt], wfc[first_chunk + i]) for i in range(PIECE_COLS // N_TILE)]
+
+        def up_relu(piece):
+            h_sb = hidden.tile([P, PIECE_COLS], F32, tag="h_sb")
+            for i, product in enumerate(handed[("product", piece)]):
+                nc.scalar.activation(out=h_sb[:, i * N_TILE : (i + 1) * N_TILE], in_=product[:], func=ACT.Relu)
+            handed[("h_sb", piece)] = h_sb
+
+        def up_square_store(piece):
+            tt, first_col = place_of_piece(piece)
+            h_sb = handed[("h_sb", piece)]
+            nc.vector.tensor_tensor(out=h_sb[:], in0=h_sb[:], in1=h_sb[:], op=ALU.mult)
+            nc.sync.dma_start(out=h_rows[tt * P : (tt + 1) * P, first_col : first_col + PIECE_COLS], in_=h_sb[:])
+
+        def when(stage_of, number, count):
+            if 0 <= number < count:
+                stage_of(number)
 
         gain = consts.tile([P, MODEL], BF16)
         for dc in range(MODEL // N_TILE):
@@ -177,63 +275,42 @@ def tile_shepherdembryo_pb_kernel(tc, y_attn, x, w_o, attn_scale, w_fc, out_0, o
             nc.tensor.matmul(out=spread[:], lhsT=ones[:], rhs=gain_row0[:, cols], start=True, stop=True)
             nc.vector.tensor_copy(out=gain[:, cols], in_=spread[:])
 
-        xn = [packed_tokens("xn%d" % tt) for tt in range(TOKEN_TILES)]
-        for tt in range(TOKEN_TILES):
-            gained = norm.tile([P, MODEL], F32, tag="gained")
-            for dc in range(MODEL // N_TILE):
-                cols = slice(dc * N_TILE, (dc + 1) * N_TILE)
-                attn_out = multiply(yc[tt], wo[dc])
-                nc.vector.tensor_tensor(out=gained[:, cols], in0=attn_out[:], in1=gain[:, cols], op=ALU.mult)
-            x_mid = mids.tile([P, MODEL], F32, tag="x_mid")
-            nc.vector.tensor_tensor(out=x_mid[:], in0=gained[:], in1=x_sb[:, tt, :], op=ALU.add)
-            nc.sync.dma_start(out=x_mid_rows[tt * P : (tt + 1) * P, :], in_=x_mid[:])
+        for unit in range(WO_UNITS):
+            flip_unit(unit)
+            copy_unit(unit)
+            when(quantise_unit, unit - 1, WO_UNITS)
+        quantise_unit(WO_UNITS - 1)
+        raw_units.extend([load_unit(w_fc, unit) for unit in range(WFC_UNITS - WO_UNITS, WFC_UNITS)])
+        for tt in range(2):
+            flip_yc(tt)
+            copy_yc(tt)
+            quantise_yc(tt)
+        project(0)
 
-            squares = norm.tile([P, MODEL], BF16, tag="squares")
-            mean_sq = norm.tile([P, 1], F32, tag="mean_sq")
-            nc.scalar.activation(
-                out=squares[:], in_=x_mid[:], func=ACT.Square, scale=MODEL**-0.5, accum_out=mean_sq[:]
-            )
-            rms = norm.tile([P, 1], F32, tag="rms")
-            nc.scalar.activation(out=rms[:], in_=mean_sq[:], func=ACT.Sqrt, bias=eps_col[:])
-            inv_rms = norm.tile([P, 1], F32, tag="inv_rms")
-            nc.vector.reciprocal(out=inv_rms[:], in_=rms[:])
-
-            xn_sorted = norm.tile([P, PASSES * HALVES, 2, P], BF16, tag="xn_sorted")
-            nc.scalar.activation(
-                out=xn_sorted[:],
-                in_=x_mid[:].rearrange("t (a p e) -> t a e p", p=P, e=2),
-                func=ACT.Copy,
-                scale=inv_rms[:],
-            )
-            bank = psum.tile([P, PASSES, PACK, P], BF16, tag="flip")
-            for g in range(PASSES):
-                for u in range(HALVES):
-                    for e in range(2):
-                        nc.tensor.transpose(bank[:, g, 2 * u + e, :], xn_sorted[:, HALVES * g + u, e, :], ident_bf16[:])
-            grouped = stage.tile([P, PASSES * P * PACK], BF16, tag="grouped", align_bytes=64)
-            nc.scalar.copy(
-                out=grouped[:].rearrange("p (g t v) -> p g t v", g=PASSES, v=PACK),
-                in_=bank[:].rearrange("p g v t -> p g t v"),
-            )
-            nc.vector.quantize_mx(out=xn[tt][0][:].bitcast(FP8X4), scales=xn[tt][1][:], in_=grouped[:])
-
-        wfc = [packed_chunk("wfc%d" % c) for c in range(WFC_UNITS // UNITS_PER_CHUNK)]
-
-        def quantise_wfc_unit(unit):
-            chunk = wfc[unit // UNITS_PER_CHUNK]
-            quantise_unit(unit, wfc_raw[unit], chunk[0], chunk[1])
-
-        def up_project(tt, first_col):
-            h_sb = hidden.tile([P, STORE_COLS], F32, tag="h_sb")
-            for col in range(0, STORE_COLS, N_TILE):
-                product = multiply(xn[tt], wfc[(first_col + col) // N_TILE])
-                nc.scalar.activation(out=h_sb[:, col : col + N_TILE], in_=product[:], func=ACT.Relu)
-            nc.vector.tensor_tensor(out=h_sb[:], in0=h_sb[:], in1=h_sb[:], op=ALU.mult)
-            nc.sync.dma_start(out=h_rows[tt * P : (tt + 1) * P, first_col : first_col + STORE_COLS], in_=h_sb[:])
-
-        for unit in range(UNITS_AHEAD):
-            quantise_wfc_unit(unit)
-        for step in range(WFC_UNITS):
-            if step + UNITS_AHEAD < WFC_UNITS:
-                quantise_wfc_unit(step + UNITS_AHEAD)
-            up_project(step % TOKEN_TILES, (step // TOKEN_TILES) * STORE_COLS)
+        for tick in range(TOKEN_TILES + PIECES + 3):
+            two_units = tick < TOKEN_TILES
+            unit = WO_UNITS + (2 * tick if two_units else tick + TOKEN_TILES)
+            when(flip_xn, tick - 2, TOKEN_TILES)
+            when(flip_unit, unit, ALL_UNITS)
+            when(root_mean_square, tick - 1, TOKEN_TILES)
+            if tick > 0:
+                when(quantise_unit, unit - 1, ALL_UNITS)
+            when(add_residual, tick, TOKEN_TILES)
+            when(invert_rms, tick - 1, TOKEN_TILES)
+            when(copy_xn, tick - 2, TOKEN_TILES)
+            when(up_multiply, tick - TOKEN_TILES, PIECES)
+            when(up_relu, tick - TOKEN_TILES - 1, PIECES)
+            when(copy_unit, unit, ALL_UNITS)
+            when(project, tick + 1, TOKEN_TILES)
+            when(flip_yc, tick + 2, TOKEN_TILES)
+            if two_units:
+                flip_unit(unit + 1)
+            when(normalise, tick - 1, TOKEN_TILES)
+            when(quantise_xn, tick - 2, TOKEN_TILES)
+            when(up_square_store, tick - TOKEN_TILES - 2, PIECES)
+            if two_units:
+                quantise_unit(unit)
+            when(copy_yc, tick + 2, TOKEN_TILES)
+            if two_units:
+                copy_unit(unit + 1)
+            when(quantise_yc, tick + 2, TOKEN_TILES)

@@ -31,7 +31,7 @@ WO_UNITS = MODEL // UNIT_ROWS
 WFC_UNITS = HIDDEN // UNIT_ROWS
 PIECE_COLS = 1024
 PIECES = TOKEN_TILES * (HIDDEN // PIECE_COLS)
-VECTOR_EVERY = 4
+DOUBLE_TICKS = 6
 
 FLOPS = 2 * TOKENS * MODEL * (MODEL + HIDDEN)
 
@@ -88,11 +88,11 @@ def tile_shepherdembryo_pb_kernel(tc, y_attn, x, w_o, attn_scale, w_fc, out_0, o
             return y_sb, x_sb
 
         raw_units = [load_unit(w_o, unit) for unit in range(WO_UNITS)]
-        token_inputs = [load_tokens(tt) for tt in range(2)]
-        for tt in range(2, TOKEN_TILES):
-            raw_units.extend([load_unit(w_fc, unit) for unit in range(2 * tt - 4, 2 * tt - 2)])
+        token_inputs = []
+        for tt in range(TOKEN_TILES):
             token_inputs.append(load_tokens(tt))
-        raw_units.extend([load_unit(w_fc, unit) for unit in range(2 * TOKEN_TILES - 4, WFC_UNITS - WO_UNITS)])
+            raw_units.extend([load_unit(w_fc, unit) for unit in range(2 * tt, 2 * tt + 2)])
+        raw_units.extend([load_unit(w_fc, unit) for unit in range(2 * TOKEN_TILES, WFC_UNITS - WO_UNITS)])
         ALL_UNITS = WO_UNITS + WFC_UNITS
 
         def packed_tokens(name):
@@ -145,7 +145,7 @@ def tile_shepherdembryo_pb_kernel(tc, y_attn, x, w_o, attn_scale, w_fc, out_0, o
                 grouped = stage.tile([P, UNIT_ROWS * PACK], BF16, tag="grouped", align_bytes=64)
                 out = grouped[:].bitcast(F32).rearrange("p (q r u) -> p q r u", r=2, u=HALVES)
                 in_ = handed[("unit bank", unit, g)][:].rearrange("p u r q -> p q r u")
-                if (PASSES * unit + g) % VECTOR_EVERY == 0:
+                if g == 0 and (unit < WO_UNITS + 2 * DOUBLE_TICKS or unit % 2 == 0):
                     nc.vector.tensor_copy(out=out, in_=in_)
                 else:
                     nc.scalar.copy(out=out, in_=in_)
@@ -268,32 +268,29 @@ def tile_shepherdembryo_pb_kernel(tc, y_attn, x, w_o, attn_scale, w_fc, out_0, o
             if 0 <= number < count:
                 stage_of(number)
 
-        gain = consts.tile([P, MODEL], BF16)
-        for dc in range(MODEL // N_TILE):
-            cols = slice(dc * N_TILE, (dc + 1) * N_TILE)
-            spread = psum.tile([P, N_TILE], F32, tag="acc")
-            nc.tensor.matmul(out=spread[:], lhsT=ones[:], rhs=gain_row0[:, cols], start=True, stop=True)
-            nc.vector.tensor_copy(out=gain[:, cols], in_=spread[:])
-
         for unit in range(WO_UNITS):
             flip_unit(unit)
             copy_unit(unit)
             when(quantise_unit, unit - 1, WO_UNITS)
         quantise_unit(WO_UNITS - 1)
         raw_units.extend([load_unit(w_fc, unit) for unit in range(WFC_UNITS - WO_UNITS, WFC_UNITS)])
-        for tt in range(2):
-            flip_yc(tt)
-            copy_yc(tt)
-            quantise_yc(tt)
-        project(0)
+        flip_yc(0)
+        copy_yc(0)
+        quantise_yc(0)
+        gain = consts.tile([P, MODEL], BF16)
+        for dc in range(MODEL // N_TILE):
+            cols = slice(dc * N_TILE, (dc + 1) * N_TILE)
+            spread = psum.tile([P, N_TILE], F32, tag="acc")
+            nc.tensor.matmul(out=spread[:], lhsT=ones[:], rhs=gain_row0[:, cols], start=True, stop=True)
+            nc.scalar.copy(out=gain[:, cols], in_=spread[:])
 
-        for tick in range(TOKEN_TILES + PIECES + 3):
-            two_units = tick < TOKEN_TILES
-            unit = WO_UNITS + (2 * tick if two_units else tick + TOKEN_TILES)
+        for tick in range(-1, TOKEN_TILES + PIECES + 3):
+            two_units = tick + 1 < DOUBLE_TICKS
+            unit = WO_UNITS + (2 * (tick + 1) if two_units else tick + 1 + DOUBLE_TICKS)
             when(flip_xn, tick - 2, TOKEN_TILES)
             when(flip_unit, unit, ALL_UNITS)
             when(root_mean_square, tick - 1, TOKEN_TILES)
-            if tick > 0:
+            if tick >= 0:
                 when(quantise_unit, unit - 1, ALL_UNITS)
             when(add_residual, tick, TOKEN_TILES)
             when(invert_rms, tick - 1, TOKEN_TILES)

@@ -140,12 +140,12 @@ def tile_shepherdembryo_pb_kernel(tc, y_attn, x, w_o, attn_scale, w_fc, out_0, o
                         nc.tensor.transpose(bank[:, u, r, :], words[:, r, first : first + P], ident_words[:])
                 handed[("unit bank", unit, g)] = bank
 
-        def copy_unit(unit):
+        def copy_unit(unit, on_vector):
             for g in range(PASSES):
                 grouped = stage.tile([P, UNIT_ROWS * PACK], BF16, tag="grouped", align_bytes=64)
                 out = grouped[:].bitcast(F32).rearrange("p (q r u) -> p q r u", r=2, u=HALVES)
                 in_ = handed[("unit bank", unit, g)][:].rearrange("p u r q -> p q r u")
-                if g == 0 and (unit < WO_UNITS + 2 * DOUBLE_TICKS or unit % 2 == 0):
+                if on_vector[g]:
                     nc.vector.tensor_copy(out=out, in_=in_)
                 else:
                     nc.scalar.copy(out=out, in_=in_)
@@ -270,7 +270,7 @@ def tile_shepherdembryo_pb_kernel(tc, y_attn, x, w_o, attn_scale, w_fc, out_0, o
 
         for unit in range(WO_UNITS):
             flip_unit(unit)
-            copy_unit(unit)
+            copy_unit(unit, [True, False])
             when(quantise_unit, unit - 1, WO_UNITS)
         quantise_unit(WO_UNITS - 1)
         raw_units.extend([load_unit(w_fc, unit) for unit in range(WFC_UNITS - WO_UNITS, WFC_UNITS)])
@@ -289,15 +289,18 @@ def tile_shepherdembryo_pb_kernel(tc, y_attn, x, w_o, attn_scale, w_fc, out_0, o
             unit = WO_UNITS + (2 * (tick + 1) if two_units else tick + 1 + DOUBLE_TICKS)
             when(flip_xn, tick - 2, TOKEN_TILES)
             when(flip_unit, unit, ALL_UNITS)
+            when(add_residual, tick, TOKEN_TILES)
             when(root_mean_square, tick - 1, TOKEN_TILES)
+            when(invert_rms, tick - 1, TOKEN_TILES)
             if tick >= 0:
                 when(quantise_unit, unit - 1, ALL_UNITS)
-            when(add_residual, tick, TOKEN_TILES)
-            when(invert_rms, tick - 1, TOKEN_TILES)
             when(copy_xn, tick - 2, TOKEN_TILES)
             when(up_multiply, tick - TOKEN_TILES, PIECES)
             when(up_relu, tick - TOKEN_TILES - 1, PIECES)
-            when(copy_unit, unit, ALL_UNITS)
+            if two_units:
+                copy_unit(unit, [0 < tick, 1 < tick])
+            elif unit < ALL_UNITS:
+                copy_unit(unit, [unit % 2 == 0, False])
             when(project, tick + 1, TOKEN_TILES)
             when(flip_yc, tick + 2, TOKEN_TILES)
             if two_units:
@@ -309,5 +312,5 @@ def tile_shepherdembryo_pb_kernel(tc, y_attn, x, w_o, attn_scale, w_fc, out_0, o
                 quantise_unit(unit)
             when(copy_yc, tick + 2, TOKEN_TILES)
             if two_units:
-                copy_unit(unit + 1)
+                copy_unit(unit + 1, [2 < tick, 3 < tick])
             when(quantise_yc, tick + 2, TOKEN_TILES)

@@ -284,9 +284,10 @@ def tile_shepherdembryo_pb_kernel(tc, y_attn, x, w_o, attn_scale, w_fc, out_0, o
             nc.tensor.matmul(out=spread[:], lhsT=ones[:], rhs=gain_row0[:, cols], start=True, stop=True)
             nc.scalar.copy(out=gain[:, cols], in_=spread[:])
 
-        for tick in range(-1, TOKEN_TILES + PIECES + 3):
+        for tick in range(-1, TOKEN_TILES + PIECES + 1):
             two_units = tick + 1 < DOUBLE_TICKS
             unit = WO_UNITS + (2 * (tick + 1) if two_units else tick + 1 + DOUBLE_TICKS)
+            when(up_multiply, tick - TOKEN_TILES, PIECES)
             when(flip_xn, tick - 2, TOKEN_TILES)
             when(flip_unit, unit, ALL_UNITS)
             when(add_residual, tick, TOKEN_TILES)
@@ -295,8 +296,6 @@ def tile_shepherdembryo_pb_kernel(tc, y_attn, x, w_o, attn_scale, w_fc, out_0, o
             if tick >= 0:
                 when(quantise_unit, unit - 1, ALL_UNITS)
             when(copy_xn, tick - 2, TOKEN_TILES)
-            when(up_multiply, tick - TOKEN_TILES, PIECES)
-            when(up_relu, tick - TOKEN_TILES - 1, PIECES)
             if two_units:
                 copy_unit(unit, [0 < tick, 1 < tick])
             elif unit < ALL_UNITS:
@@ -306,11 +305,12 @@ def tile_shepherdembryo_pb_kernel(tc, y_attn, x, w_o, attn_scale, w_fc, out_0, o
             if two_units:
                 flip_unit(unit + 1)
             when(normalise, tick - 1, TOKEN_TILES)
+            when(up_relu, tick - TOKEN_TILES, PIECES)
             when(quantise_xn, tick - 2, TOKEN_TILES)
-            when(up_square_store, tick - TOKEN_TILES - 2, PIECES)
             if two_units:
                 quantise_unit(unit)
             when(copy_yc, tick + 2, TOKEN_TILES)
             if two_units:
                 copy_unit(unit + 1, [2 < tick, 3 < tick])
             when(quantise_yc, tick + 2, TOKEN_TILES)
+            when(up_square_store, tick - TOKEN_TILES - 1, PIECES)

@@ -56,7 +56,6 @@ def tile_shepherdembryo_pb_kernel(tc, y_attn, x, w_o, attn_scale, w_fc, out_0, o
 
         gain_row0 = consts.tile([P, MODEL], BF16)
         nc.vector.memset(gain_row0[:], 0.0)
-        nc.scalar.dma_start(out=gain_row0[0:1, :], in_=attn_scale.rearrange("(o d) -> o d", o=1))
         ones = consts.tile([P, P], BF16)
         nc.vector.memset(ones[:], 1.0)
         eps_col = consts.tile([P, 1], F32)
@@ -65,8 +64,6 @@ def tile_shepherdembryo_pb_kernel(tc, y_attn, x, w_o, attn_scale, w_fc, out_0, o
         nc.scalar.activation(out=table_warmer[:], in_=eps_col[:], func=ACT.Sqrt)
         ident_words = consts.tile([P, P], F32)
         make_identity(nc, ident_words[:])
-        ident_bf16 = consts.tile([P, P], BF16)
-        make_identity(nc, ident_bf16[:])
 
         def load_unit(w, unit):
             raw = weights.tile([P, 2, MODEL], BF16, tag="raw")
@@ -76,23 +73,30 @@ def tile_shepherdembryo_pb_kernel(tc, y_attn, x, w_o, attn_scale, w_fc, out_0, o
             )
             return raw
 
-        def load_tokens(tt):
+        def load_yc(tt):
             b, s0 = divmod(tt * P, SEQ)
             y_sb = inputs.tile([P, MODEL], BF16, name="y_sb%d" % tt)
             nc.sync.dma_start(
                 out=y_sb[:].rearrange("s (h j) -> s h j", h=HEADS),
                 in_=y_attn[b, :, s0 : s0 + P, :].rearrange("h s j -> s h j"),
             )
+            return y_sb
+
+        def load_x(tt):
             x_sb = inputs.tile([P, MODEL], BF16, name="x_sb%d" % tt)
             nc.sync.dma_start(out=x_sb[:], in_=x_rows[tt * P : (tt + 1) * P, :])
-            return y_sb, x_sb
+            return x_sb
 
+        y_tiles = [load_yc(0)]
+        nc.sync.dma_start(out=gain_row0[0:1, :], in_=attn_scale.rearrange("(o d) -> o d", o=1))
         raw_units = [load_unit(w_o, unit) for unit in range(WO_UNITS)]
-        token_inputs = []
-        for tt in range(TOKEN_TILES):
-            token_inputs.append(load_tokens(tt))
-            raw_units.extend([load_unit(w_fc, unit) for unit in range(2 * tt, 2 * tt + 2)])
-        raw_units.extend([load_unit(w_fc, unit) for unit in range(2 * TOKEN_TILES, WFC_UNITS - WO_UNITS)])
+        x_tiles = [load_x(0)]
+        for tt in range(1, TOKEN_TILES):
+            raw_units.append(load_unit(w_fc, 2 * tt - 2))
+            y_tiles.append(load_yc(tt))
+            raw_units.append(load_unit(w_fc, 2 * tt - 1))
+            x_tiles.append(load_x(tt))
+        raw_units.extend([load_unit(w_fc, unit) for unit in range(2 * TOKEN_TILES - 2, WFC_UNITS - WO_UNITS)])
         ALL_UNITS = WO_UNITS + WFC_UNITS
 
         def packed_tokens(name):
@@ -162,22 +166,28 @@ def tile_shepherdembryo_pb_kernel(tc, y_attn, x, w_o, attn_scale, w_fc, out_0, o
                     in_=handed[("unit grouped", unit, g)][:],
                 )
 
-        def flip_yc(tt):
-            words = token_inputs[tt][0][:].bitcast(F32)
+        def flip_words(rows):
+            words = rows[:].bitcast(F32)
             bank = psum.tile([P, PASSES, HALVES, P], F32, tag="flip")
             for g in range(PASSES):
                 for u in range(HALVES):
                     first = (HALVES * g + u) * P
                     nc.tensor.transpose(bank[:, g, u, :], words[:, first : first + P], ident_words[:])
-            handed[("yc bank", tt)] = bank
+            return bank
 
-        def copy_yc(tt):
+        def copy_words(bank):
             grouped = stage.tile([P, PASSES * P * PACK], BF16, tag="grouped", align_bytes=64)
             nc.scalar.copy(
                 out=grouped[:].bitcast(F32).rearrange("p (g t u) -> p g t u", g=PASSES, u=HALVES),
-                in_=handed[("yc bank", tt)][:].rearrange("p g u t -> p g t u"),
+                in_=bank[:].rearrange("p g u t -> p g t u"),
             )
-            handed[("yc grouped", tt)] = grouped
+            return grouped
+
+        def flip_yc(tt):
+            handed[("yc bank", tt)] = flip_words(y_tiles[tt])
+
+        def copy_yc(tt):
+            handed[("yc grouped", tt)] = copy_words(handed[("yc bank", tt)])
 
         def quantise_yc(tt):
             nc.vector.quantize_mx(
@@ -187,13 +197,19 @@ def tile_shepherdembryo_pb_kernel(tc, y_attn, x, w_o, attn_scale, w_fc, out_0, o
         def project(tt):
             handed[("attn_out", tt)] = [multiply(yc[tt], wo[dc]) for dc in range(MODEL // N_TILE)]
 
-        def add_residual(tt):
+        halves = [slice(dc * N_TILE, (dc + 1) * N_TILE) for dc in range(MODEL // N_TILE)]
+
+        def apply_gain(tt):
             gained = norm.tile([P, MODEL], F32, tag="gained")
-            for dc, attn_out in enumerate(handed[("attn_out", tt)]):
-                cols = slice(dc * N_TILE, (dc + 1) * N_TILE)
+            for attn_out, cols in zip(handed[("attn_out", tt)], halves):
                 nc.vector.tensor_tensor(out=gained[:, cols], in0=attn_out[:], in1=gain[:, cols], op=ALU.mult)
+            handed[("gained", tt)] = gained
+
+        def add_residual(tt):
+            gained = handed[("gained", tt)]
             x_mid = mids.tile([P, MODEL], F32, tag="x_mid")
-            nc.vector.tensor_tensor(out=x_mid[:], in0=gained[:], in1=token_inputs[tt][1][:], op=ALU.add)
+            for cols in halves:
+                nc.vector.tensor_tensor(out=x_mid[:, cols], in0=gained[:, cols], in1=x_tiles[tt][:, cols], op=ALU.add)
             nc.sync.dma_start(out=x_mid_rows[tt * P : (tt + 1) * P, :], in_=x_mid[:])
             handed[("x_mid", tt)] = x_mid
 
@@ -203,6 +219,10 @@ def tile_shepherdembryo_pb_kernel(tc, y_attn, x, w_o, attn_scale, w_fc, out_0, o
             nc.scalar.activation(
                 out=squares[:], in_=handed[("x_mid", tt)][:], func=ACT.Square, scale=MODEL**-0.5, accum_out=mean_sq[:]
             )
+            handed[("mean_sq", tt)] = mean_sq
+
+        def root(tt):
+            mean_sq = handed[("mean_sq", tt)]
             rms = norm.tile([P, 1], F32, tag="rms")
             nc.scalar.activation(out=rms[:], in_=mean_sq[:], func=ACT.Sqrt, bias=eps_col[:])
             handed[("rms", tt)] = rms
@@ -213,31 +233,17 @@ def tile_shepherdembryo_pb_kernel(tc, y_attn, x, w_o, attn_scale, w_fc, out_0, o
             handed[("inv_rms", tt)] = inv_rms
 
         def normalise(tt):
-            xn_sorted = norm.tile([P, PASSES * HALVES, 2, P], BF16, tag="xn_sorted")
+            xn_rows = norm.tile([P, MODEL], BF16, tag="xn_rows")
             nc.scalar.activation(
-                out=xn_sorted[:],
-                in_=handed[("x_mid", tt)][:].rearrange("t (a p e) -> t a e p", p=P, e=2),
-                func=ACT.Copy,
-                scale=handed[("inv_rms", tt)][:],
+                out=xn_rows[:], in_=handed[("x_mid", tt)][:], func=ACT.Copy, scale=handed[("inv_rms", tt)][:]
             )
-            handed[("xn_sorted", tt)] = xn_sorted
+            handed[("xn rows", tt)] = xn_rows
 
         def flip_xn(tt):
-            xn_sorted = handed[("xn_sorted", tt)]
-            bank = psum.tile([P, PASSES, PACK, P], BF16, tag="flip")
-            for g in range(PASSES):
-                for u in range(HALVES):
-                    for e in range(2):
-                        nc.tensor.transpose(bank[:, g, 2 * u + e, :], xn_sorted[:, HALVES * g + u, e, :], ident_bf16[:])
-            handed[("xn bank", tt)] = bank
+            handed[("xn bank", tt)] = flip_words(handed[("xn rows", tt)])
 
         def copy_xn(tt):
-            grouped = stage.tile([P, PASSES * P * PACK], BF16, tag="grouped", align_bytes=64)
-            nc.scalar.copy(
-                out=grouped[:].rearrange("p (g t v) -> p g t v", g=PASSES, v=PACK),
-                in_=handed[("xn bank", tt)][:].rearrange("p g v t -> p g t v"),
-            )
-            handed[("xn grouped", tt)] = grouped
+            handed[("xn grouped", tt)] = copy_words(handed[("xn bank", tt)])
 
         def quantise_xn(tt):
             nc.vector.quantize_mx(
@@ -268,49 +274,53 @@ def tile_shepherdembryo_pb_kernel(tc, y_attn, x, w_o, attn_scale, w_fc, out_0, o
             if 0 <= number < count:
                 stage_of(number)
 
+        flip_yc(0)
+        copy_yc(0)
+        quantise_yc(0)
         for unit in range(WO_UNITS):
             flip_unit(unit)
             copy_unit(unit, [True, False])
             when(quantise_unit, unit - 1, WO_UNITS)
-        quantise_unit(WO_UNITS - 1)
+            if unit == 2:
+                gain = consts.tile([P, MODEL], BF16)
+                for dc in range(MODEL // N_TILE):
+                    cols = slice(dc * N_TILE, (dc + 1) * N_TILE)
+                    spread = psum.tile([P, N_TILE], F32, tag="acc")
+                    nc.tensor.matmul(out=spread[:], lhsT=ones[:], rhs=gain_row0[:, cols], start=True, stop=True)
+                    nc.scalar.copy(out=gain[:, cols], in_=spread[:])
         raw_units.extend([load_unit(w_fc, unit) for unit in range(WFC_UNITS - WO_UNITS, WFC_UNITS)])
-        flip_yc(0)
-        copy_yc(0)
-        quantise_yc(0)
-        gain = consts.tile([P, MODEL], BF16)
-        for dc in range(MODEL // N_TILE):
-            cols = slice(dc * N_TILE, (dc + 1) * N_TILE)
-            spread = psum.tile([P, N_TILE], F32, tag="acc")
-            nc.tensor.matmul(out=spread[:], lhsT=ones[:], rhs=gain_row0[:, cols], start=True, stop=True)
-            nc.scalar.copy(out=gain[:, cols], in_=spread[:])
-
+        quantise_unit(WO_UNITS - 1)
+        VB = {-1: 2, 1: 1, 2: 1, 3: 1, 4: 3, 5: 1, 7: 1}
         for tick in range(-1, TOKEN_TILES + PIECES + 1):
             two_units = tick + 1 < DOUBLE_TICKS
             unit = WO_UNITS + (2 * (tick + 1) if two_units else tick + 1 + DOUBLE_TICKS)
+            vb = VB.get(tick, 0)
+            on_v = [i < vb for i in range(4)]
             when(up_multiply, tick - TOKEN_TILES, PIECES)
+            when(project, tick + 1, 1 if tick < 0 else 0)
             when(flip_xn, tick - 2, TOKEN_TILES)
             when(flip_unit, unit, ALL_UNITS)
-            when(add_residual, tick, TOKEN_TILES)
             when(root_mean_square, tick - 1, TOKEN_TILES)
-            when(invert_rms, tick - 1, TOKEN_TILES)
+            when(apply_gain, tick, TOKEN_TILES)
             if tick >= 0:
                 when(quantise_unit, unit - 1, ALL_UNITS)
             when(copy_xn, tick - 2, TOKEN_TILES)
-            if two_units:
-                copy_unit(unit, [0 < tick, 1 < tick])
-            elif unit < ALL_UNITS:
-                copy_unit(unit, [unit % 2 == 0, False])
-            when(project, tick + 1, TOKEN_TILES)
+            when(root, tick - 1, TOKEN_TILES)
+            when(invert_rms, tick - 1, TOKEN_TILES)
+            when(add_residual, tick, TOKEN_TILES)
+            if unit < ALL_UNITS:
+                copy_unit(unit, on_v[0:2])
+            when(project, tick + 1, TOKEN_TILES if tick >= 0 else 0)
             when(flip_yc, tick + 2, TOKEN_TILES)
             if two_units:
                 flip_unit(unit + 1)
-            when(normalise, tick - 1, TOKEN_TILES)
             when(up_relu, tick - TOKEN_TILES, PIECES)
+            when(normalise, tick - 1, TOKEN_TILES)
             when(quantise_xn, tick - 2, TOKEN_TILES)
-            if two_units:
-                quantise_unit(unit)
             when(copy_yc, tick + 2, TOKEN_TILES)
             if two_units:
-                copy_unit(unit + 1, [2 < tick, 3 < tick])
+                quantise_unit(unit)
+            if two_units:
+                copy_unit(unit + 1, on_v[2:4])
             when(quantise_yc, tick + 2, TOKEN_TILES)
             when(up_square_store, tick - TOKEN_TILES - 1, PIECES)

@@ -234,8 +234,8 @@ def tile_shepherdembryo_pb_kernel(tc, y_attn, x, w_o, attn_scale, w_fc, out_0, o
 
         def normalise(tt):
             xn_rows = norm.tile([P, MODEL], BF16, tag="xn_rows")
-            nc.scalar.activation(
-                out=xn_rows[:], in_=handed[("x_mid", tt)][:], func=ACT.Copy, scale=handed[("inv_rms", tt)][:]
+            nc.vector.tensor_scalar(
+                out=xn_rows[:], in0=handed[("x_mid", tt)][:], scalar1=handed[("inv_rms", tt)][:], scalar2=None, op0=ALU.mult
             )
             handed[("xn rows", tt)] = xn_rows
 
@@ -290,7 +290,7 @@ def tile_shepherdembryo_pb_kernel(tc, y_attn, x, w_o, attn_scale, w_fc, out_0, o
                     nc.scalar.copy(out=gain[:, cols], in_=spread[:])
         raw_units.extend([load_unit(w_fc, unit) for unit in range(WFC_UNITS - WO_UNITS, WFC_UNITS)])
         quantise_unit(WO_UNITS - 1)
-        VB = {-1: 2, 1: 1, 2: 1, 3: 1, 4: 3, 5: 1, 7: 1}
+        VB = {-1: 1, 4: 1, 5: 1, 6: 1}
         for tick in range(-1, TOKEN_TILES + PIECES + 1):
             two_units = tick + 1 < DOUBLE_TICKS
             unit = WO_UNITS + (2 * (tick + 1) if two_units else tick + 1 + DOUBLE_TICKS)

@@ -297,9 +297,10 @@ def tile_shepherdembryo_pb_kernel(tc, y_attn, x, w_o, attn_scale, w_fc, out_0, o
             vb = VB.get(tick, 0)
             on_v = [i < vb for i in range(4)]
             when(up_multiply, tick - TOKEN_TILES, PIECES)
-            when(project, tick + 1, 1 if tick < 0 else 0)
             when(flip_xn, tick - 2, TOKEN_TILES)
             when(flip_unit, unit, ALL_UNITS)
+            when(flip_yc, tick + 2, TOKEN_TILES)
+            when(project, tick + 1, 1)
             when(root_mean_square, tick - 1, TOKEN_TILES)
             when(apply_gain, tick, TOKEN_TILES)
             if tick >= 0:
@@ -310,11 +311,10 @@ def tile_shepherdembryo_pb_kernel(tc, y_attn, x, w_o, attn_scale, w_fc, out_0, o
             when(add_residual, tick, TOKEN_TILES)
             if unit < ALL_UNITS:
                 copy_unit(unit, on_v[0:2])
-            when(project, tick + 1, TOKEN_TILES if tick >= 0 else 0)
-            when(flip_yc, tick + 2, TOKEN_TILES)
             if two_units:
                 flip_unit(unit + 1)
-            when(up_relu, tick - TOKEN_TILES, PIECES)
+            if tick >= 0:
+                when(project, tick + 1, TOKEN_TILES)
             when(normalise, tick - 1, TOKEN_TILES)
             when(quantise_xn, tick - 2, TOKEN_TILES)
             when(copy_yc, tick + 2, TOKEN_TILES)
@@ -322,5 +322,6 @@ def tile_shepherdembryo_pb_kernel(tc, y_attn, x, w_o, attn_scale, w_fc, out_0, o
                 quantise_unit(unit)
             if two_units:
                 copy_unit(unit + 1, on_v[2:4])
+            when(up_relu, tick - TOKEN_TILES, PIECES)
             when(quantise_yc, tick + 2, TOKEN_TILES)
             when(up_square_store, tick - TOKEN_TILES - 1, PIECES)

@@ -12,8 +12,9 @@ ALU = mybir.AluOpType
 ACT = mybir.ActivationFunctionType
 
 P = 128
-SEQ = 256
 HEADS = 8
+HEAD_DIM = 128
+PAIR = 2
 TOKENS = 512
 MODEL = 1024
 HIDDEN = 4096
@@ -38,9 +39,8 @@ FLOPS = 2 * TOKENS * MODEL * (MODEL + HIDDEN)
 
 def tile_shepherdembryo_pb_kernel(tc, y_attn, x, w_o, attn_scale, w_fc, out_0, out_1):
     nc = tc.nc
-    x_rows = x.flatten_outer_dims()
-    x_mid_rows = out_0.flatten_outer_dims()
-    h_rows = out_1.flatten_outer_dims()
+    x_mid_rows = out_0.rearrange("b (p r) d -> b r p d", r=PAIR)
+    h_rows = out_1.rearrange("b (p r) f -> b r p f", r=PAIR)
 
     with ExitStack() as ctx:
         consts = ctx.enter_context(tc.tile_pool(name="consts", bufs=1))
@@ -73,30 +73,31 @@ def tile_shepherdembryo_pb_kernel(tc, y_attn, x, w_o, attn_scale, w_fc, out_0, o
             )
             return raw
 
-        def load_yc(tt):
-            b, s0 = divmod(tt * P, SEQ)
-            y_sb = inputs.tile([P, MODEL], BF16, name="y_sb%d" % tt)
+        def load_yc(b):
+            y_sb = inputs.tile([P, HEADS, PAIR, HEAD_DIM], BF16, name="y_sb%d" % b)
             nc.sync.dma_start(
-                out=y_sb[:].rearrange("s (h j) -> s h j", h=HEADS),
-                in_=y_attn[b, :, s0 : s0 + P, :].rearrange("h s j -> s h j"),
+                out=y_sb[:].rearrange("p h r j -> p h (r j)"), in_=y_attn[b].rearrange("h (p r) j -> p h (r j)", r=PAIR)
             )
             return y_sb
 
-        def load_x(tt):
-            x_sb = inputs.tile([P, MODEL], BF16, name="x_sb%d" % tt)
-            nc.sync.dma_start(out=x_sb[:], in_=x_rows[tt * P : (tt + 1) * P, :])
+        def load_x(b):
+            x_sb = inputs.tile([P, PAIR, MODEL], BF16, name="x_sb%d" % b)
+            nc.sync.dma_start(
+                out=x_sb[:].rearrange("p r d -> p (r d)"), in_=x[b].rearrange("(p r) d -> p (r d)", r=PAIR)
+            )
             return x_sb
 
-        y_tiles = [load_yc(0)]
+        raw_units = [load_unit(w_o, 0)]
         nc.sync.dma_start(out=gain_row0[0:1, :], in_=attn_scale.rearrange("(o d) -> o d", o=1))
-        raw_units = [load_unit(w_o, unit) for unit in range(WO_UNITS)]
+        y_tiles = [load_yc(0)]
+        raw_units.extend([load_unit(w_o, unit) for unit in range(1, WO_UNITS)])
+        raw_units.append(load_unit(w_fc, 0))
+        y_tiles.append(load_yc(1))
+        raw_units.extend([load_unit(w_fc, unit) for unit in range(1, 3)])
         x_tiles = [load_x(0)]
-        for tt in range(1, TOKEN_TILES):
-            raw_units.append(load_unit(w_fc, 2 * tt - 2))
-            y_tiles.append(load_yc(tt))
-            raw_units.append(load_unit(w_fc, 2 * tt - 1))
-            x_tiles.append(load_x(tt))
-        raw_units.extend([load_unit(w_fc, unit) for unit in range(2 * TOKEN_TILES - 2, WFC_UNITS - WO_UNITS)])
+        raw_units.extend([load_unit(w_fc, unit) for unit in range(3, 6)])
+        x_tiles.append(load_x(1))
+        raw_units.extend([load_unit(w_fc, unit) for unit in range(6, WFC_UNITS - WO_UNITS)])
         ALL_UNITS = WO_UNITS + WFC_UNITS
 
         def packed_tokens(name):
@@ -183,8 +184,15 @@ def tile_shepherdembryo_pb_kernel(tc, y_attn, x, w_o, attn_scale, w_fc, out_0, o
             )
             return grouped
 
+        def sort_yc(tt):
+            y_rows = inputs.tile([P, MODEL], BF16, name="y_rows%d" % tt)
+            out = y_rows[:].rearrange("p (h j) -> p h j", h=HEADS)
+            in_ = y_tiles[tt // PAIR][:, :, tt % PAIR, :]
+            nc.vector.tensor_copy(out=out, in_=in_)
+            handed[("yc rows", tt)] = y_rows
+
         def flip_yc(tt):
-            handed[("yc bank", tt)] = flip_words(y_tiles[tt])
+            handed[("yc bank", tt)] = flip_words(handed[("yc rows", tt)])
 
         def copy_yc(tt):
             handed[("yc grouped", tt)] = copy_words(handed[("yc bank", tt)])
@@ -208,9 +216,8 @@ def tile_shepherdembryo_pb_kernel(tc, y_attn, x, w_o, attn_scale, w_fc, out_0, o
         def add_residual(tt):
             gained = handed[("gained", tt)]
             x_mid = mids.tile([P, MODEL], F32, tag="x_mid")
-            for cols in halves:
-                nc.vector.tensor_tensor(out=x_mid[:, cols], in0=gained[:, cols], in1=x_tiles[tt][:, cols], op=ALU.add)
-            nc.sync.dma_start(out=x_mid_rows[tt * P : (tt + 1) * P, :], in_=x_mid[:])
+            nc.vector.tensor_tensor(out=x_mid[:], in0=gained[:], in1=x_tiles[tt // PAIR][:, tt % PAIR, :], op=ALU.add)
+            nc.sync.dma_start(out=x_mid_rows[tt // PAIR, tt % PAIR], in_=x_mid[:])
             handed[("x_mid", tt)] = x_mid
 
         def root_mean_square(tt):
@@ -268,19 +275,24 @@ def tile_shepherdembryo_pb_kernel(tc, y_attn, x, w_o, attn_scale, w_fc, out_0, o
             tt, first_col = place_of_piece(piece)
             h_sb = handed[("h_sb", piece)]
             nc.vector.tensor_tensor(out=h_sb[:], in0=h_sb[:], in1=h_sb[:], op=ALU.mult)
-            nc.sync.dma_start(out=h_rows[tt * P : (tt + 1) * P, first_col : first_col + PIECE_COLS], in_=h_sb[:])
+            nc.sync.dma_start(out=h_rows[tt // PAIR, tt % PAIR, :, first_col : first_col + PIECE_COLS], in_=h_sb[:])
 
         def when(stage_of, number, count):
             if 0 <= number < count:
                 stage_of(number)
 
-        flip_yc(0)
-        copy_yc(0)
-        quantise_yc(0)
         for unit in range(WO_UNITS):
             flip_unit(unit)
             copy_unit(unit, [True, False])
+            if unit == 0:
+                sort_yc(0)
+                flip_yc(0)
             when(quantise_unit, unit - 1, WO_UNITS)
+            if unit == 0:
+                copy_yc(0)
+                quantise_yc(0)
+            if unit == 1:
+                sort_yc(1)
             if unit == 2:
                 gain = consts.tile([P, MODEL], BF16)
                 for dc in range(MODEL // N_TILE):
@@ -299,6 +311,8 @@ def tile_shepherdembryo_pb_kernel(tc, y_attn, x, w_o, attn_scale, w_fc, out_0, o
             when(up_multiply, tick - TOKEN_TILES, PIECES)
             when(flip_xn, tick - 2, TOKEN_TILES)
             when(flip_unit, unit, ALL_UNITS)
+            if tick >= 0:
+                when(sort_yc, tick + 2, TOKEN_TILES)
             when(flip_yc, tick + 2, TOKEN_TILES)
             when(project, tick + 1, 1)
             when(root_mean_square, tick - 1, TOKEN_TILES)

@@ -93,11 +93,11 @@ def tile_shepherdembryo_pb_kernel(tc, y_attn, x, w_o, attn_scale, w_fc, out_0, o
         raw_units.extend([load_unit(w_o, unit) for unit in range(1, WO_UNITS)])
         raw_units.append(load_unit(w_fc, 0))
         y_tiles.append(load_yc(1))
-        raw_units.extend([load_unit(w_fc, unit) for unit in range(1, 3)])
+        raw_units.append(load_unit(w_fc, 1))
         x_tiles = [load_x(0)]
-        raw_units.extend([load_unit(w_fc, unit) for unit in range(3, 6)])
+        raw_units.extend([load_unit(w_fc, unit) for unit in range(2, 5)])
         x_tiles.append(load_x(1))
-        raw_units.extend([load_unit(w_fc, unit) for unit in range(6, WFC_UNITS - WO_UNITS)])
+        raw_units.extend([load_unit(w_fc, unit) for unit in range(5, WFC_UNITS - WO_UNITS)])
         ALL_UNITS = WO_UNITS + WFC_UNITS
 
         def packed_tokens(name):
@@ -302,40 +302,46 @@ def tile_shepherdembryo_pb_kernel(tc, y_attn, x, w_o, attn_scale, w_fc, out_0, o
                     nc.scalar.copy(out=gain[:, cols], in_=spread[:])
         raw_units.extend([load_unit(w_fc, unit) for unit in range(WFC_UNITS - WO_UNITS, WFC_UNITS)])
         quantise_unit(WO_UNITS - 1)
-        VB = {-1: 1, 4: 1, 5: 1, 6: 1}
+        VB = {-1: 1, 4: 1, 5: 2, 8: 1}
+        next_unit = WO_UNITS
+        pending = None
         for tick in range(-1, TOKEN_TILES + PIECES + 1):
-            two_units = tick + 1 < DOUBLE_TICKS
-            unit = WO_UNITS + (2 * (tick + 1) if two_units else tick + 1 + DOUBLE_TICKS)
+            count = min(2 if 1 <= tick <= 5 else 1, ALL_UNITS - next_unit)
+            units = list(range(next_unit, next_unit + count))
+            next_unit += count
             vb = VB.get(tick, 0)
             on_v = [i < vb for i in range(4)]
             when(up_multiply, tick - TOKEN_TILES, PIECES)
             when(flip_xn, tick - 2, TOKEN_TILES)
-            when(flip_unit, unit, ALL_UNITS)
+            if count > 0:
+                flip_unit(units[0])
             if tick >= 0:
                 when(sort_yc, tick + 2, TOKEN_TILES)
             when(flip_yc, tick + 2, TOKEN_TILES)
             when(project, tick + 1, 1)
             when(root_mean_square, tick - 1, TOKEN_TILES)
             when(apply_gain, tick, TOKEN_TILES)
-            if tick >= 0:
-                when(quantise_unit, unit - 1, ALL_UNITS)
+            if pending is not None:
+                quantise_unit(pending)
+                pending = None
             when(copy_xn, tick - 2, TOKEN_TILES)
             when(root, tick - 1, TOKEN_TILES)
             when(invert_rms, tick - 1, TOKEN_TILES)
             when(add_residual, tick, TOKEN_TILES)
-            if unit < ALL_UNITS:
-                copy_unit(unit, on_v[0:2])
-            if two_units:
-                flip_unit(unit + 1)
+            if count > 0:
+                copy_unit(units[0], on_v[0:2])
+                pending = units[0]
+            if count > 1:
+                flip_unit(units[1])
             if tick >= 0:
                 when(project, tick + 1, TOKEN_TILES)
             when(normalise, tick - 1, TOKEN_TILES)
             when(quantise_xn, tick - 2, TOKEN_TILES)
             when(copy_yc, tick + 2, TOKEN_TILES)
-            if two_units:
-                quantise_unit(unit)
-            if two_units:
-                copy_unit(unit + 1, on_v[2:4])
+            if count > 1:
+                quantise_unit(units[0])
+                copy_unit(units[1], on_v[2:4])
+                pending = units[1]
             when(up_relu, tick - TOKEN_TILES, PIECES)
             when(quantise_yc, tick + 2, TOKEN_TILES)
             when(up_square_store, tick - TOKEN_TILES - 1, PIECES)

@@ -32,7 +32,6 @@ WO_UNITS = MODEL // UNIT_ROWS
 WFC_UNITS = HIDDEN // UNIT_ROWS
 PIECE_COLS = 1024
 PIECES = TOKEN_TILES * (HIDDEN // PIECE_COLS)
-DOUBLE_TICKS = 6
 
 FLOPS = 2 * TOKENS * MODEL * (MODEL + HIDDEN)
 
@@ -50,7 +49,7 @@ def tile_shepherdembryo_pb_kernel(tc, y_attn, x, w_o, attn_scale, w_fc, out_0, o
         stage = ctx.enter_context(tc.tile_pool(name="stage", bufs=6))
         norm = ctx.enter_context(tc.tile_pool(name="norm", bufs=2))
         mids = ctx.enter_context(tc.tile_pool(name="mids", bufs=TOKEN_TILES))
-        hidden = ctx.enter_context(tc.tile_pool(name="hidden", bufs=6))
+        hidden = ctx.enter_context(tc.tile_pool(name="hidden", bufs=8))
         psum = ctx.enter_context(tc.psum_pool(name="psum", bufs=4))
         ctx.enter_context(tc.manual_schedule())
 
@@ -91,11 +90,10 @@ def tile_shepherdembryo_pb_kernel(tc, y_attn, x, w_o, attn_scale, w_fc, out_0, o
         nc.sync.dma_start(out=gain_row0[0:1, :], in_=attn_scale.rearrange("(o d) -> o d", o=1))
         y_tiles = [load_yc(0)]
         raw_units.extend([load_unit(w_o, unit) for unit in range(1, WO_UNITS)])
-        raw_units.append(load_unit(w_fc, 0))
         y_tiles.append(load_yc(1))
-        raw_units.append(load_unit(w_fc, 1))
+        raw_units.append(load_unit(w_fc, 0))
         x_tiles = [load_x(0)]
-        raw_units.extend([load_unit(w_fc, unit) for unit in range(2, 5)])
+        raw_units.extend([load_unit(w_fc, unit) for unit in range(1, 5)])
         x_tiles.append(load_x(1))
         raw_units.extend([load_unit(w_fc, unit) for unit in range(5, WFC_UNITS - WO_UNITS)])
         ALL_UNITS = WO_UNITS + WFC_UNITS
@@ -302,11 +300,11 @@ def tile_shepherdembryo_pb_kernel(tc, y_attn, x, w_o, attn_scale, w_fc, out_0, o
                     nc.scalar.copy(out=gain[:, cols], in_=spread[:])
         raw_units.extend([load_unit(w_fc, unit) for unit in range(WFC_UNITS - WO_UNITS, WFC_UNITS)])
         quantise_unit(WO_UNITS - 1)
-        VB = {-1: 1, 4: 1, 5: 2, 8: 1}
+        VB = {4: 1, 5: 2, 6: 1, 9: 1}
         next_unit = WO_UNITS
         pending = None
         for tick in range(-1, TOKEN_TILES + PIECES + 1):
-            count = min(2 if 1 <= tick <= 5 else 1, ALL_UNITS - next_unit)
+            count = min(0 if tick < 0 else 2 if 1 <= tick <= 5 else 1, ALL_UNITS - next_unit)
             units = list(range(next_unit, next_unit + count))
             next_unit += count
             vb = VB.get(tick, 0)

from contextlib import ExitStack

import concourse.mybir as mybir
from concourse.masks import make_identity

F32 = mybir.dt.float32
BF16 = mybir.dt.bfloat16
U32 = mybir.dt.uint32
U8 = mybir.dt.uint8
FP8X4 = mybir.dt.float8_e4m3fn_x4
ALU = mybir.AluOpType
ACT = mybir.ActivationFunctionType

P = 128
HEADS = 8
HEAD_DIM = 128
PAIR = 2
TOKENS = 512
MODEL = 1024
HIDDEN = 4096
EPS = 1e-6

PACK = 4
K_PASS = P * PACK
PASSES = MODEL // K_PASS
HALVES = 2
TOKEN_TILES = TOKENS // P
N_TILE = 512
UNIT_ROWS = 2 * P
UNITS_PER_CHUNK = N_TILE // UNIT_ROWS
WO_UNITS = MODEL // UNIT_ROWS
WFC_UNITS = HIDDEN // UNIT_ROWS
PIECE_COLS = 1024
PIECES = TOKEN_TILES * (HIDDEN // PIECE_COLS)

FLOPS = 2 * TOKENS * MODEL * (MODEL + HIDDEN)


def tile_shepherdembryo_pb_kernel(tc, y_attn, x, w_o, attn_scale, w_fc, out_0, out_1):
    nc = tc.nc
    x_mid_rows = out_0.rearrange("b (p r) d -> b r p d", r=PAIR)
    h_rows = out_1.rearrange("b (p r) f -> b r p f", r=PAIR)

    with ExitStack() as ctx:
        consts = ctx.enter_context(tc.tile_pool(name="consts", bufs=1))
        inputs = ctx.enter_context(tc.tile_pool(name="inputs", bufs=1))
        weights = ctx.enter_context(tc.tile_pool(name="weights", bufs=WFC_UNITS))
        packed = ctx.enter_context(tc.tile_pool(name="packed", bufs=1))
        stage = ctx.enter_context(tc.tile_pool(name="stage", bufs=6))
        norm = ctx.enter_context(tc.tile_pool(name="norm", bufs=2))
        mids = ctx.enter_context(tc.tile_pool(name="mids", bufs=TOKEN_TILES))
        hidden = ctx.enter_context(tc.tile_pool(name="hidden", bufs=8))
        psum = ctx.enter_context(tc.psum_pool(name="psum", bufs=4))
        ctx.enter_context(tc.manual_schedule())

        gain_row0 = consts.tile([P, MODEL], BF16)
        nc.vector.memset(gain_row0[:], 0.0)
        ones = consts.tile([P, P], BF16)
        nc.vector.memset(ones[:], 1.0)
        eps_col = consts.tile([P, 1], F32)
        nc.vector.memset(eps_col[:], EPS)
        table_warmer = consts.tile([P, 1], F32)
        nc.scalar.activation(out=table_warmer[:], in_=eps_col[:], func=ACT.Sqrt)
        ident_words = consts.tile([P, P], F32)
        make_identity(nc, ident_words[:])

        def load_unit(w, unit):
            raw = weights.tile([P, 2, MODEL], BF16, tag="raw")
            nc.sync.dma_start(
                out=raw[:].rearrange("p r k -> p (r k)"),
                in_=w[unit * UNIT_ROWS : (unit + 1) * UNIT_ROWS, :].rearrange("(p r) k -> p (r k)", r=2),
            )
            return raw

        def load_yc(b):
            y_sb = inputs.tile([P, HEADS, PAIR, HEAD_DIM], BF16, name="y_sb%d" % b)
            nc.sync.dma_start(
                out=y_sb[:].rearrange("p h r j -> p h (r j)"), in_=y_attn[b].rearrange("h (p r) j -> p h (r j)", r=PAIR)
            )
            return y_sb

        def load_x(b):
            x_sb = inputs.tile([P, PAIR, MODEL], BF16, name="x_sb%d" % b)
            nc.sync.dma_start(
                out=x_sb[:].rearrange("p r d -> p (r d)"), in_=x[b].rearrange("(p r) d -> p (r d)", r=PAIR)
            )
            return x_sb

        raw_units = [load_unit(w_o, 0)]
        nc.sync.dma_start(out=gain_row0[0:1, :], in_=attn_scale.rearrange("(o d) -> o d", o=1))
        y_tiles = [load_yc(0)]
        raw_units.extend([load_unit(w_o, unit) for unit in range(1, WO_UNITS)])
        y_tiles.append(load_yc(1))
        raw_units.append(load_unit(w_fc, 0))
        x_tiles = [load_x(0)]
        raw_units.extend([load_unit(w_fc, unit) for unit in range(1, 5)])
        x_tiles.append(load_x(1))
        raw_units.extend([load_unit(w_fc, unit) for unit in range(5, WFC_UNITS - WO_UNITS)])
        ALL_UNITS = WO_UNITS + WFC_UNITS

        def packed_tokens(name):
            codes = packed.tile([P, PASSES * P], U32, name=name + "_codes", align_bytes=64)
            scales = packed.tile([P, PASSES * P], U8, name=name + "_scales", align_bytes=64)
            return codes, scales

        def packed_chunk(name):
            codes = packed.tile([P, PASSES, N_TILE], U32, name=name + "_codes", align_bytes=64)
            scales = packed.tile([P, PASSES, N_TILE], U8, name=name + "_scales", align_bytes=64)
            return codes, scales

        yc = [packed_tokens("yc%d" % tt) for tt in range(TOKEN_TILES)]
        xn = [packed_tokens("xn%d" % tt) for tt in range(TOKEN_TILES)]
        chunks = [packed_chunk("w%d" % c) for c in range(ALL_UNITS // UNITS_PER_CHUNK)]
        wo = chunks[: WO_UNITS // UNITS_PER_CHUNK]
        wfc = chunks[WO_UNITS // UNITS_PER_CHUNK :]

        def multiply(tokens, chunk):
            t_codes, t_scales = tokens
            c_codes, c_scales = chunk
            acc = psum.tile([P, N_TILE], F32, tag="acc")
            for g in range(PASSES):
                t_cols = slice(g * P, (g + 1) * P)
                nc.tensor.matmul_mx(
                    out=acc[:],
                    lhsT=t_codes[:, t_cols].bitcast(FP8X4),
                    lhsT_scale=t_scales[:, t_cols],
                    rhs=c_codes[:, g, :].bitcast(FP8X4),
                    rhs_scale=c_scales[:, g, :],
                    start=(g == 0),
                    stop=(g == PASSES - 1),
                )
            return acc

        handed = {}

        def flip_unit(unit):
            words = raw_units[unit][:].bitcast(F32)
            for g in range(PASSES):
                bank = psum.tile([P, HALVES, 2, P], F32, tag="flip")
                for u in range(HALVES):
                    first = (HALVES * g + u) * P
                    for r in range(2):
                        nc.tensor.transpose(bank[:, u, r, :], words[:, r, first : first + P], ident_words[:])
                handed[("unit bank", unit, g)] = bank

        def copy_unit(unit, on_vector):
            for g in range(PASSES):
                grouped = stage.tile([P, UNIT_ROWS * PACK], BF16, tag="grouped", align_bytes=64)
                out = grouped[:].bitcast(F32).rearrange("p (q r u) -> p q r u", r=2, u=HALVES)
                in_ = handed[("unit bank", unit, g)][:].rearrange("p u r q -> p q r u")
                if on_vector[g]:
                    nc.vector.tensor_copy(out=out, in_=in_)
                else:
                    nc.scalar.copy(out=out, in_=in_)
                handed[("unit grouped", unit, g)] = grouped

        def quantise_unit(unit):
            codes, scales = chunks[unit // UNITS_PER_CHUNK]
            first_col = (unit % UNITS_PER_CHUNK) * UNIT_ROWS
            cols = slice(first_col, first_col + UNIT_ROWS)
            for g in range(PASSES):
                nc.vector.quantize_mx(
                    out=codes[:, g, cols].bitcast(FP8X4),
                    scales=scales[:, g, cols],
                    in_=handed[("unit grouped", unit, g)][:],
                )

        def flip_words(rows):
            words = rows[:].bitcast(F32)
            bank = psum.tile([P, PASSES, HALVES, P], F32, tag="flip")
            for g in range(PASSES):
                for u in range(HALVES):
                    first = (HALVES * g + u) * P
                    nc.tensor.transpose(bank[:, g, u, :], words[:, first : first + P], ident_words[:])
            return bank

        def copy_words(bank):
            grouped = stage.tile([P, PASSES * P * PACK], BF16, tag="grouped", align_bytes=64)
            nc.scalar.copy(
                out=grouped[:].bitcast(F32).rearrange("p (g t u) -> p g t u", g=PASSES, u=HALVES),
                in_=bank[:].rearrange("p g u t -> p g t u"),
            )
            return grouped

        def sort_yc(tt):
            y_rows = inputs.tile([P, MODEL], BF16, name="y_rows%d" % tt)
            out = y_rows[:].rearrange("p (h j) -> p h j", h=HEADS)
            in_ = y_tiles[tt // PAIR][:, :, tt % PAIR, :]
            nc.vector.tensor_copy(out=out, in_=in_)
            handed[("yc rows", tt)] = y_rows

        def flip_yc(tt):
            handed[("yc bank", tt)] = flip_words(handed[("yc rows", tt)])

        def copy_yc(tt):
            handed[("yc grouped", tt)] = copy_words(handed[("yc bank", tt)])

        def quantise_yc(tt):
            nc.vector.quantize_mx(
                out=yc[tt][0][:].bitcast(FP8X4), scales=yc[tt][1][:], in_=handed[("yc grouped", tt)][:]
            )

        def project(tt):
            handed[("attn_out", tt)] = [multiply(yc[tt], wo[dc]) for dc in range(MODEL // N_TILE)]

        halves = [slice(dc * N_TILE, (dc + 1) * N_TILE) for dc in range(MODEL // N_TILE)]

        def apply_gain(tt):
            gained = norm.tile([P, MODEL], F32, tag="gained")
            for attn_out, cols in zip(handed[("attn_out", tt)], halves):
                nc.vector.tensor_tensor(out=gained[:, cols], in0=attn_out[:], in1=gain[:, cols], op=ALU.mult)
            handed[("gained", tt)] = gained

        def add_residual(tt):
            gained = handed[("gained", tt)]
            x_mid = mids.tile([P, MODEL], F32, tag="x_mid")
            nc.vector.tensor_tensor(out=x_mid[:], in0=gained[:], in1=x_tiles[tt // PAIR][:, tt % PAIR, :], op=ALU.add)
            nc.sync.dma_start(out=x_mid_rows[tt // PAIR, tt % PAIR], in_=x_mid[:])
            handed[("x_mid", tt)] = x_mid

        def root_mean_square(tt):
            squares = norm.tile([P, MODEL], BF16, tag="squares")
            mean_sq = norm.tile([P, 1], F32, tag="mean_sq")
            nc.scalar.activation(
                out=squares[:], in_=handed[("x_mid", tt)][:], func=ACT.Square, scale=MODEL**-0.5, accum_out=mean_sq[:]
            )
            handed[("mean_sq", tt)] = mean_sq

        def root(tt):
            mean_sq = handed[("mean_sq", tt)]
            rms = norm.tile([P, 1], F32, tag="rms")
            nc.scalar.activation(out=rms[:], in_=mean_sq[:], func=ACT.Sqrt, bias=eps_col[:])
            handed[("rms", tt)] = rms

        def invert_rms(tt):
            inv_rms = norm.tile([P, 1], F32, tag="inv_rms")
            nc.vector.reciprocal(out=inv_rms[:], in_=handed[("rms", tt)][:])
            handed[("inv_rms", tt)] = inv_rms

        def normalise(tt):
            xn_rows = norm.tile([P, MODEL], BF16, tag="xn_rows")
            nc.vector.tensor_scalar(
                out=xn_rows[:], in0=handed[("x_mid", tt)][:], scalar1=handed[("inv_rms", tt)][:], scalar2=None, op0=ALU.mult
            )
            handed[("xn rows", tt)] = xn_rows

        def flip_xn(tt):
            handed[("xn bank", tt)] = flip_words(handed[("xn rows", tt)])

        def copy_xn(tt):
            handed[("xn grouped", tt)] = copy_words(handed[("xn bank", tt)])

        def quantise_xn(tt):
            nc.vector.quantize_mx(
                out=xn[tt][0][:].bitcast(FP8X4), scales=xn[tt][1][:], in_=handed[("xn grouped", tt)][:]
            )

        def place_of_piece(piece):
            return piece % TOKEN_TILES, (piece // TOKEN_TILES) * PIECE_COLS

        def up_multiply(piece):
            tt, first_col = place_of_piece(piece)
            first_chunk = first_col // N_TILE
            handed[("product", piece)] = [multiply(xn[tt], wfc[first_chunk + i]) for i in range(PIECE_COLS // N_TILE)]

        def up_relu(piece):
            h_sb = hidden.tile([P, PIECE_COLS], F32, tag="h_sb")
            for i, product in enumerate(handed[("product", piece)]):
                nc.scalar.activation(out=h_sb[:, i * N_TILE : (i + 1) * N_TILE], in_=product[:], func=ACT.Relu)
            handed[("h_sb", piece)] = h_sb

        def up_square_store(piece):
            tt, first_col = place_of_piece(piece)
            h_sb = handed[("h_sb", piece)]
            nc.vector.tensor_tensor(out=h_sb[:], in0=h_sb[:], in1=h_sb[:], op=ALU.mult)
            nc.sync.dma_start(out=h_rows[tt // PAIR, tt % PAIR, :, first_col : first_col + PIECE_COLS], in_=h_sb[:])

        def when(stage_of, number, count):
            if 0 <= number < count:
                stage_of(number)

        for unit in range(WO_UNITS):
            flip_unit(unit)
            copy_unit(unit, [True, False])
            if unit == 0:
                sort_yc(0)
                flip_yc(0)
            when(quantise_unit, unit - 1, WO_UNITS)
            if unit == 0:
                copy_yc(0)
                quantise_yc(0)
            if unit == 1:
                sort_yc(1)
            if unit == 2:
                gain = consts.tile([P, MODEL], BF16)
                for dc in range(MODEL // N_TILE):
                    cols = slice(dc * N_TILE, (dc + 1) * N_TILE)
                    spread = psum.tile([P, N_TILE], F32, tag="acc")
                    nc.tensor.matmul(out=spread[:], lhsT=ones[:], rhs=gain_row0[:, cols], start=True, stop=True)
                    nc.scalar.copy(out=gain[:, cols], in_=spread[:])
        raw_units.extend([load_unit(w_fc, unit) for unit in range(WFC_UNITS - WO_UNITS, WFC_UNITS)])
        quantise_unit(WO_UNITS - 1)
        VB = {4: 1, 5: 2, 6: 1, 9: 1}
        next_unit = WO_UNITS
        pending = None
        for tick in range(-1, TOKEN_TILES + PIECES + 1):
            count = min(0 if tick < 0 else 2 if 1 <= tick <= 5 else 1, ALL_UNITS - next_unit)
            units = list(range(next_unit, next_unit + count))
            next_unit += count
            vb = VB.get(tick, 0)
            on_v = [i < vb for i in range(4)]
            when(up_multiply, tick - TOKEN_TILES, PIECES)
            when(flip_xn, tick - 2, TOKEN_TILES)
            if count > 0:
                flip_unit(units[0])
            if tick >= 0:
                when(sort_yc, tick + 2, TOKEN_TILES)
            when(flip_yc, tick + 2, TOKEN_TILES)
            when(project, tick + 1, 1)
            when(root_mean_square, tick - 1, TOKEN_TILES)
            when(apply_gain, tick, TOKEN_TILES)
            if pending is not None:
                quantise_unit(pending)
                pending = None
            when(copy_xn, tick - 2, TOKEN_TILES)
            when(root, tick - 1, TOKEN_TILES)
            when(invert_rms, tick - 1, TOKEN_TILES)
            when(add_residual, tick, TOKEN_TILES)
            if count > 0:
                copy_unit(units[0], on_v[0:2])
                pending = units[0]
            if count > 1:
                flip_unit(units[1])
            if tick >= 0:
                when(project, tick + 1, TOKEN_TILES)
            when(normalise, tick - 1, TOKEN_TILES)
            when(quantise_xn, tick - 2, TOKEN_TILES)
            when(copy_yc, tick + 2, TOKEN_TILES)
            if count > 1:
                quantise_unit(units[0])
                copy_unit(units[1], on_v[2:4])
                pending = units[1]
            when(up_relu, tick - TOKEN_TILES, PIECES)
            when(quantise_yc, tick + 2, TOKEN_TILES)
            when(up_square_store, tick - TOKEN_TILES - 1, PIECES)
